import numpy as np
import ml_dtypes


BF16 = ml_dtypes.bfloat16


def bf(x):
    return np.asarray(x, np.float32).astype(BF16)


def f64(x):
    return np.asarray(x).astype(np.float64)


E2M1 = np.array([0.0, 0.5, 1.0, 1.5, 2.0, 3.0, 4.0, 6.0, -0.0, -0.5, -1.0, -1.5, -2.0, -3.0, -4.0, -6.0])


def pack_weight(w, fmt):
    k, n = w.shape
    w = f64(bf(w)).reshape(k // 32, 32, n)
    amax = np.abs(w).max(1)
    if fmt == "e4m3":
        byte = np.frexp(amax)[1] - 1 + 127 - 7
    else:
        mant, ex = np.frexp(amax / 6.0)
        byte = np.where(mant > 0.5, ex, ex - 1) + 127
    byte = np.clip(np.where(amax > 0, byte, 1), 1, 254)
    scaled = (w * np.exp2(127.0 - byte)[:, None, :]).reshape(k, n).astype(np.float32)
    by_word = np.ascontiguousarray(scaled.reshape(k // 512, 128, 4, n).transpose(0, 1, 3, 2))
    if fmt == "e4m3":
        words = by_word.astype(ml_dtypes.float8_e4m3fn).view(np.uint8)
    else:
        c = by_word.astype(ml_dtypes.float4_e2m1fn).view(np.uint8) & 0xF
        words = c[..., 0::2] | (c[..., 1::2] << 4)
    return np.ascontiguousarray(words), np.ascontiguousarray(byte.astype(np.uint8).reshape(k // 512, 16, n))


def unpack_weight(words, scales, fmt):
    g, p, n, _ = words.shape
    if fmt == "e4m3":
        vals = np.ascontiguousarray(words).view(ml_dtypes.float8_e4m3fn).astype(np.float64)
    else:
        nib = np.empty((g, p, n, 4), np.uint8)
        nib[..., 0::2] = words & 0xF
        nib[..., 1::2] = words >> 4
        vals = E2M1[nib]
    vals = vals * np.repeat(np.exp2(scales.astype(np.float64) - 127.0), 8, axis=1)[..., None]
    return vals.transpose(0, 1, 3, 2).reshape(g * 512, n)

def pack4(w):
    words, scales = pack_weight(w, "e2m1")
    return words.reshape(words.shape[0], 128, -1), scales


def unpack4(words, scales):
    return unpack_weight(words.reshape(words.shape[0], 128, -1, 2), scales, "e2m1")


def kspread(k):
    return np.exp2(np.repeat(np.random.randint(-6, 7, k // 32), 32).astype(np.float64))


B, T, C, E, DV, R, G, BLK = 1, 1536, 4096, 1536, 1536, 16, 16, 512
BASE = 1e4


def rope(x):
    inv_freq = 1.0 / (BASE ** (f64(np.arange(0, R, 2)) / R))
    ang = f64(np.arange(T))[:, None] * inv_freq[None, :]
    ang = np.repeat(ang, 2, axis=-1)
    cos, sin = np.cos(ang), np.sin(ang)
    xl, xr = x[..., :R], x[..., R:]
    p = xl.reshape(xl.shape[:-1] + (R // 2, 2))
    rot = np.stack((-p[..., 1], p[..., 0]), axis=-1).reshape(xl.shape)
    return np.concatenate([xl * cos + rot * sin, xr], axis=-1)


def setup_inputs():
    s = kspread(C)
    Q_in = np.random.standard_normal((B, T, C)) * s
    Q_in_words, Q_in_scales = pack4(np.ascontiguousarray(Q_in.reshape(B * T, C).T))
    wq_words, wq_scales = pack4(np.random.standard_normal((C, E)) * 0.25 / np.sqrt(C) / s[:, None])
    wk_words, wk_scales = pack4(np.random.standard_normal((C, E)) * 0.25 / np.sqrt(C) / s[:, None])
    return {"Q_in_words": Q_in_words, "Q_in_scales": Q_in_scales,
            "W_Q_words": wq_words, "W_Q_scales": wq_scales,
            "W_K_words": wk_words, "W_K_scales": wk_scales}


def reference(Q_in_words, Q_in_scales, W_Q_words, W_Q_scales, W_K_words, W_K_scales):
    xq = unpack4(Q_in_words, Q_in_scales).T.reshape(B, T, C)
    q = rope(xq @ unpack4(W_Q_words, W_Q_scales))
    k = rope(xq @ unpack4(W_K_words, W_K_scales))
    return q, k

@@ -1,0 +1,223 @@
+import math
+from contextlib import ExitStack
+
+import concourse.mybir as mybir
+
+F32 = mybir.dt.float32
+BF16 = mybir.dt.bfloat16
+I32 = mybir.dt.int32
+U8 = mybir.dt.uint8
+FP4X4 = mybir.dt.float4_e2m1fn_x4
+ALU = mybir.AluOpType
+ACT = mybir.ActivationFunctionType
+
+P = 128
+TOKENS, CHANNELS, OUT = 1536, 4096, 1536
+PASSES = CHANNELS // 512
+N_TILE = 512
+TOKEN_TILES = TOKENS // P
+ROPE = 16
+PAIRS = ROPE // 2
+BASE = 1e4
+WARM = 10
+
+FLOPS = 2 * TOKENS * CHANNELS * 2 * OUT
+
+
+def load_codes(nc, block, words, g0, g1):
+    codes, planes, c0 = block
+    nbytes = codes.shape[2]
+    nc.sync.dma_start(
+        out=codes[:, g0:g1, :].bitcast(I32),
+        in_=words[g0:g1, :, 2 * c0 : 2 * c0 + nbytes].rearrange("g p b -> p g b").bitcast(I32),
+    )
+
+
+def load_scales(nc, block, scales, g0, g1, quadrants=(0, 1, 2, 3)):
+    codes, planes, c0 = block
+    width = planes.shape[2]
+    for q in quadrants:
+        nc.sync.dma_start(
+            out=planes[32 * q : 32 * q + 4, g0:g1, :].bitcast(I32),
+            in_=scales[g0:g1, 4 * q : 4 * q + 4, c0 : c0 + width].rearrange("g r n -> r g n").bitcast(I32),
+        )
+
+
+def zero_planes(nc, block, g0, g1):
+    codes, planes, c0 = block
+    nc.vector.memset(planes[:, g0:g1, :].bitcast(I32), 0)
+
+
+def tile_wqkv_pa_kernel(tc, q_words, q_scales, wq_words, wq_scales, wk_words, wk_scales, out_q, out_k):
+    nc = tc.nc
+    with ExitStack() as ctx:
+        keep = ctx.enter_context(tc.tile_pool(name="keep", bufs=1))
+        results = ctx.enter_context(tc.tile_pool(name="results", bufs=8))
+        small = ctx.enter_context(tc.tile_pool(name="small", bufs=4))
+        psum = ctx.enter_context(tc.psum_pool(name="psum", bufs=8))
+        ctx.enter_context(tc.manual_schedule())
+
+        def make_block(name, c0, width):
+            codes = keep.tile([P, PASSES, 2 * width], U8, name=name + "_codes", align_bytes=256)
+            planes = keep.tile([P, PASSES, width], U8, name=name + "_planes", align_bytes=256)
+            return codes, planes, c0
+
+        xa = make_block("xa", 0, 512)
+        xb = make_block("xb", 512, 1024)
+        wq0 = make_block("wq0", 0, 1024)
+        wq1 = make_block("wq1", 1024, 512)
+        wk = make_block("wk", 0, 1536)
+
+        ones = keep.tile([P, N_TILE], BF16, name="ones", align_bytes=64)
+        nc.gpsimd.memset(ones[:], 1.0)
+        pos = keep.tile([P, TOKEN_TILES], I32, name="pos")
+        nc.gpsimd.iota(pos[:], pattern=[[P, TOKEN_TILES]], base=0, channel_multiplier=1)
+
+        zero_planes(nc, xa, 0, 2)
+        zero_planes(nc, wq0, 0, 2)
+        zero_planes(nc, xa, 2, 4)
+        zero_planes(nc, wq0, 2, 4)
+        zero_planes(nc, xa, 4, 8)
+        zero_planes(nc, wq0, 4, 8)
+        for block in (wq1, wk, xb):
+            zero_planes(nc, block, 0, 8)
+
+        load_codes(nc, xa, q_words, 0, 1)
+        load_scales(nc, xa, q_scales, 0, 2, (0,))
+        load_codes(nc, wq0, wq_words, 0, 1)
+        load_scales(nc, xa, q_scales, 0, 2, (1, 2, 3))
+        load_scales(nc, wq0, wq_scales, 0, 2)
+        load_codes(nc, xa, q_words, 1, 2)
+        load_codes(nc, wq0, wq_words, 1, 2)
+        load_scales(nc, xa, q_scales, 2, 4)
+        load_scales(nc, wq0, wq_scales, 2, 4)
+        load_codes(nc, xa, q_words, 2, 4)
+        load_codes(nc, wq0, wq_words, 2, 4)
+        load_scales(nc, xa, q_scales, 4, 8)
+        load_scales(nc, wq0, wq_scales, 4, 8)
+        for g in (4, 6):
+            load_codes(nc, xa, q_words, g, g + 2)
+            load_codes(nc, wq0, wq_words, g, g + 2)
+        load_scales(nc, wq1, wq_scales, 0, 8)
+        for g in (0, 4):
+            load_codes(nc, wq1, wq_words, g, g + 4)
+        load_scales(nc, wk, wk_scales, 0, 8)
+        for g in (0, 2, 4, 6):
+            load_codes(nc, wk, wk_words, g, g + 2)
+        load_scales(nc, xb, q_scales, 0, 8)
+        for g in (0, 2, 4, 6):
+            load_codes(nc, xb, q_words, g, g + 2)
+
+        turns = keep.tile([P, 2, TOKEN_TILES, PAIRS], F32, name="turns")
+        for j in range(PAIRS):
+            per_pos = BASE ** (-2.0 * j / ROPE) / (2.0 * math.pi)
+            nc.vector.tensor_scalar(out=turns[:, 0, :, j], in0=pos[:], scalar1=per_pos, scalar2=None, op0=ALU.mult)
+        nc.vector.tensor_scalar(out=turns[:, 1, :, :], in0=turns[:, 0, :, :], scalar1=0.75, scalar2=None, op0=ALU.add)
+        whole = keep.tile([P, 2, TOKEN_TILES, PAIRS], I32, name="whole")
+        nc.vector.tensor_copy(out=whole[:], in_=turns[:])
+        whole_f = keep.tile([P, 2, TOKEN_TILES, PAIRS], F32, name="whole_f")
+        nc.vector.tensor_copy(out=whole_f[:], in_=whole[:])
+        part = keep.tile([P, 2, TOKEN_TILES, PAIRS], F32, name="part")
+        nc.vector.tensor_tensor(out=part[:], in0=turns[:], in1=whole_f[:], op=ALU.subtract)
+        over = keep.tile([P, 2, TOKEN_TILES, PAIRS], F32, name="over")
+        nc.vector.tensor_scalar(out=over[:], in0=part[:], scalar1=0.5, scalar2=None, op0=ALU.is_gt)
+        near = keep.tile([P, 2, TOKEN_TILES, PAIRS], F32, name="near")
+        nc.vector.tensor_tensor(out=near[:], in0=part[:], in1=over[:], op=ALU.subtract)
+        dist = keep.tile([P, 2, TOKEN_TILES, PAIRS], F32, name="dist")
+        nc.vector.scalar_tensor_tensor(out=dist[:], in0=near[:], scalar=-1.0, in1=near[:], op0=ALU.mult, op1=ALU.max)
+        folded = keep.tile([P, 2, TOKEN_TILES, PAIRS], F32, name="folded")
+        nc.vector.tensor_scalar(out=folded[:], in0=dist[:], scalar1=-1.0, scalar2=0.25, op0=ALU.mult, op1=ALU.add)
+        cos = keep.tile([P, TOKEN_TILES, PAIRS, 2], F32, name="cos")
+        sin = keep.tile([P, TOKEN_TILES, PAIRS, 2], F32, name="sin")
+        full = 2.0 * math.pi
+        nc.scalar.activation(out=cos[:, :, :, 0], in_=folded[:, 0, :, :], func=ACT.Sin, scale=full)
+        nc.scalar.activation(out=cos[:, :, :, 1], in_=folded[:, 0, :, :], func=ACT.Sin, scale=full)
+        nc.scalar.activation(out=sin[:, :, :, 0], in_=folded[:, 1, :, :], func=ACT.Sin, scale=-full)
+        nc.scalar.activation(out=sin[:, :, :, 1], in_=folded[:, 1, :, :], func=ACT.Sin, scale=full)
+
+        warm = psum.tile([P, N_TILE], F32, name="acc")
+        for w in range(WARM):
+            nc.tensor.matmul(out=warm[:], lhsT=ones[:, 0:P], rhs=ones[:], start=True, stop=True)
+
+        def mx_pass(acc, i, wblock, c, n, g):
+            xblock = xa if i < 4 else xb
+            m = P * i - xblock[2]
+            c = c - wblock[2]
+            nc.tensor.matmul_mx(
+                out=acc[:, 0:n],
+                lhsT=xblock[0][:, g, 2 * m : 2 * (m + P)].bitcast(FP4X4),
+                lhsT_scale=xblock[1][:, g, m : m + P],
+                rhs=wblock[0][:, g, 2 * c : 2 * (c + n)].bitcast(FP4X4),
+                rhs_scale=wblock[1][:, g, c : c + n],
+                start=(g == 0),
+                stop=(g == PASSES - 1),
+            )
+
+        def rope_out(acc, row, i):
+            nc.vector.tensor_copy(out=row[:, ROPE:N_TILE], in_=acc[:, ROPE:N_TILE])
+            pairs = acc[:, 0:ROPE].rearrange("p (j t) -> p j t", t=2)
+            straight = small.tile([P, PAIRS, 2], F32, name="straight")
+            nc.vector.tensor_tensor(out=straight[:], in0=pairs, in1=cos[:, i, :, :], op=ALU.mult)
+            crossed = small.tile([P, PAIRS, 2], F32, name="crossed")
+            nc.vector.tensor_tensor(out=crossed[:], in0=pairs[:, :, ::-1], in1=sin[:, i, :, :], op=ALU.mult)
+            nc.vector.tensor_tensor(out=row[:, 0:ROPE].rearrange("p (j t) -> p j t", t=2), in0=straight[:], in1=crossed[:], op=ALU.add)
+
+        def new_acc():
+            return psum.tile([P, N_TILE], F32, name="acc")
+
+        def new_row():
+            return results.tile([P, OUT], F32, name="row")
+
+        rows = [new_row() for i in range(4)]
+        accs = {}
+        for i in range(4):
+            for c in (0, 512):
+                accs[i, c] = new_acc()
+        for g in range(PASSES):
+            for i in range(4):
+                for c in (0, 512):
+                    mx_pass(accs[i, c], i, wq0, c, N_TILE, g)
+        for i in range(4):
+            rope_out(accs[i, 0], rows[i], i)
+            nc.scalar.copy(out=rows[i][:, 512:1024], in_=accs[i, 512][:])
+
+        def group(i, wblock, c, n):
+            acc = new_acc()
+            for g in range(PASSES):
+                mx_pass(acc, i, wblock, c, n, g)
+            return acc
+
+        for i in range(TOKEN_TILES):
+            t = slice(P * i, P * (i + 1))
+            if i < 4:
+                row = rows[i]
+            else:
+                row = new_row()
+                acc = group(i, wq0, 0, N_TILE)
+                rope_out(acc, row, i)
+                acc = group(i, wq0, 512, N_TILE)
+                nc.scalar.copy(out=row[:, 512:1024], in_=acc[:])
+            acc = group(i, wq1, 1024, N_TILE)
+            nc.scalar.copy(out=row[:, 1024:1536], in_=acc[:])
+            nc.sync.dma_start(out=out_q[0, t, :], in_=row[:])
+
+            row = new_row()
+            acc = group(i, wk, 0, N_TILE)
+            rope_out(acc, row, i)
+            acc = group(i, wk, 512, N_TILE)
+            nc.scalar.copy(out=row[:, 512:1024], in_=acc[:])
+            if i < TOKEN_TILES - 1:
+                acc = group(i, wk, 1024, N_TILE)
+                nc.scalar.copy(out=row[:, 1024:1536], in_=acc[:])
+                nc.sync.dma_start(out=out_k[0, t, :], in_=row[:])
+            else:
+                nc.sync.dma_start(out=out_k[0, t, 0:1024], in_=row[:, 0:1024])
+                acc = group(i, wk, 1024, 256)
+                nc.scalar.copy(out=row[:, 1024:1280], in_=acc[:, 0:256])
+                nc.sync.dma_start(out=out_k[0, t, 1024:1280], in_=row[:, 1024:1280])
+                acc = group(i, wk, 1280, 128)
+                nc.scalar.copy(out=row[:, 1280:1408], in_=acc[:, 0:128])
+                nc.sync.dma_start(out=out_k[0, t, 1280:1408], in_=row[:, 1280:1408])
+                acc = group(i, wk, 1408, 128)
+                nc.vector.tensor_copy(out=row[:, 1408:1536], in_=acc[:, 0:128])
+                nc.sync.dma_start(out=out_k[0, t, 1408:1536], in_=row[:, 1408:1536])

@@ -33,19 +33,19 @@ def load_codes(nc, block, words, g0, g1):
     )
 
 
-def load_scales(nc, block, scales, g0, g1, quadrants=(0, 1, 2, 3)):
+def load_scales(nc, block, scales, g0, g1):
     codes, planes, c0 = block
     width = planes.shape[2]
-    for q in quadrants:
+    for q in range(4):
         nc.sync.dma_start(
             out=planes[32 * q : 32 * q + 4, g0:g1, :].bitcast(I32),
             in_=scales[g0:g1, 4 * q : 4 * q + 4, c0 : c0 + width].rearrange("g r n -> r g n").bitcast(I32),
         )
 
 
-def zero_planes(nc, block, g0, g1):
+def zero_planes(engine, block, g0, g1):
     codes, planes, c0 = block
-    nc.vector.memset(planes[:, g0:g1, :].bitcast(I32), 0)
+    engine.memset(planes[:, g0:g1, :].bitcast(I32), 0)
 
 
 def tile_wqkv_pa_kernel(tc, q_words, q_scales, wq_words, wq_scales, wk_words, wk_scales, out_q, out_k):
@@ -62,51 +62,42 @@ def tile_wqkv_pa_kernel(tc, q_words, q_scales, wq_words, wq_scales, wk_words, wk
             planes = keep.tile([P, PASSES, width], U8, name=name + "_planes", align_bytes=256)
             return codes, planes, c0
 
-        xa = make_block("xa", 0, 512)
-        xb = make_block("xb", 512, 1024)
+        xs = [make_block("x" + str(n), 512 * n, 512) for n in range(3)]
         wq0 = make_block("wq0", 0, 1024)
         wq1 = make_block("wq1", 1024, 512)
-        wk = make_block("wk", 0, 1536)
+        wk0 = make_block("wk0", 0, 1024)
+        wk1 = make_block("wk1", 1024, 512)
 
+        zero_planes(nc.gpsimd, xs[0], 0, 5)
+        zero_planes(nc.vector, wq0, 0, 3)
         ones = keep.tile([P, N_TILE], BF16, name="ones", align_bytes=64)
-        nc.gpsimd.memset(ones[:], 1.0)
+        nc.vector.memset(ones[:], 1.0)
         pos = keep.tile([P, TOKEN_TILES], I32, name="pos")
         nc.gpsimd.iota(pos[:], pattern=[[P, TOKEN_TILES]], base=0, channel_multiplier=1)
+        zero_planes(nc.vector, wq0, 3, 6)
+        zero_planes(nc.vector, xs[0], 5, 8)
+        zero_planes(nc.vector, wq0, 6, 8)
+        for block in (xs[1], xs[2], wq1, wk0, wk1):
+            zero_planes(nc.vector, block, 0, 8)
 
-        zero_planes(nc, xa, 0, 2)
-        zero_planes(nc, wq0, 0, 2)
-        zero_planes(nc, xa, 2, 4)
-        zero_planes(nc, wq0, 2, 4)
-        zero_planes(nc, xa, 4, 8)
-        zero_planes(nc, wq0, 4, 8)
-        for block in (wq1, wk, xb):
-            zero_planes(nc, block, 0, 8)
+        def load_pair(g0, g1):
+            load_codes(nc, xs[0], q_words, g0, g1)
+            load_codes(nc, wq0, wq_words, g0, g1)
 
-        load_codes(nc, xa, q_words, 0, 1)
-        load_scales(nc, xa, q_scales, 0, 2, (0,))
-        load_codes(nc, wq0, wq_words, 0, 1)
-        load_scales(nc, xa, q_scales, 0, 2, (1, 2, 3))
-        load_scales(nc, wq0, wq_scales, 0, 2)
-        load_codes(nc, xa, q_words, 1, 2)
-        load_codes(nc, wq0, wq_words, 1, 2)
-        load_scales(nc, xa, q_scales, 2, 4)
-        load_scales(nc, wq0, wq_scales, 2, 4)
-        load_codes(nc, xa, q_words, 2, 4)
-        load_codes(nc, wq0, wq_words, 2, 4)
-        load_scales(nc, xa, q_scales, 4, 8)
-        load_scales(nc, wq0, wq_scales, 4, 8)
-        for g in (4, 6):
-            load_codes(nc, xa, q_words, g, g + 2)
-            load_codes(nc, wq0, wq_words, g, g + 2)
-        load_scales(nc, wq1, wq_scales, 0, 8)
-        for g in (0, 4):
-            load_codes(nc, wq1, wq_words, g, g + 4)
-        load_scales(nc, wk, wk_scales, 0, 8)
-        for g in (0, 2, 4, 6):
-            load_codes(nc, wk, wk_words, g, g + 2)
-        load_scales(nc, xb, q_scales, 0, 8)
-        for g in (0, 2, 4, 6):
-            load_codes(nc, xb, q_words, g, g + 2)
+        load_pair(0, 1)
+        load_scales(nc, xs[0], q_scales, 0, 5)
+        load_scales(nc, wq0, wq_scales, 0, 3)
+        load_pair(1, 2)
+        load_pair(2, 4)
+        load_scales(nc, wq0, wq_scales, 3, 6)
+        load_pair(4, 6)
+        load_scales(nc, xs[0], q_scales, 5, 8)
+        load_scales(nc, wq0, wq_scales, 6, 8)
+        load_pair(6, 8)
+        for block, words, scales in ((xs[1], q_words, q_scales), (xs[2], q_words, q_scales), (wq1, wq_words, wq_scales), (wk0, wk_words, wk_scales), (wk1, wk_words, wk_scales)):
+            load_scales(nc, block, scales, 0, 8)
+            load_codes(nc, block, words, 0, 4)
+            load_codes(nc, block, words, 4, 8)
 
         turns = keep.tile([P, 2, TOKEN_TILES, PAIRS], F32, name="turns")
         for j in range(PAIRS):
@@ -140,9 +131,8 @@ def tile_wqkv_pa_kernel(tc, q_words, q_scales, wq_words, wq_scales, wk_words, wk
             nc.tensor.matmul(out=warm[:], lhsT=ones[:, 0:P], rhs=ones[:], start=True, stop=True)
 
         def mx_pass(acc, i, wblock, c, n, g):
-            xblock = xa if i < 4 else xb
-            m = P * i - xblock[2]
-            c = c - wblock[2]
+            xblock = xs[i // 4]
+            m = P * (i % 4)
             nc.tensor.matmul_mx(
                 out=acc[:, 0:n],
                 lhsT=xblock[0][:, g, 2 * m : 2 * (m + P)].bitcast(FP4X4),
@@ -165,59 +155,47 @@ def tile_wqkv_pa_kernel(tc, q_words, q_scales, wq_words, wq_scales, wk_words, wk
         def new_acc():
             return psum.tile([P, N_TILE], F32, name="acc")
 
-        def new_row():
-            return results.tile([P, OUT], F32, name="row")
-
-        rows = [new_row() for i in range(4)]
-        accs = {}
-        for i in range(4):
-            for c in (0, 512):
-                accs[i, c] = new_acc()
-        for g in range(PASSES):
-            for i in range(4):
-                for c in (0, 512):
-                    mx_pass(accs[i, c], i, wq0, c, N_TILE, g)
-        for i in range(4):
-            rope_out(accs[i, 0], rows[i], i)
-            nc.scalar.copy(out=rows[i][:, 512:1024], in_=accs[i, 512][:])
-
         def group(i, wblock, c, n):
             acc = new_acc()
             for g in range(PASSES):
                 mx_pass(acc, i, wblock, c, n, g)
             return acc
 
-        for i in range(TOKEN_TILES):
-            t = slice(P * i, P * (i + 1))
-            if i < 4:
-                row = rows[i]
-            else:
-                row = new_row()
-                acc = group(i, wq0, 0, N_TILE)
-                rope_out(acc, row, i)
-                acc = group(i, wq0, 512, N_TILE)
-                nc.scalar.copy(out=row[:, 512:1024], in_=acc[:])
-            acc = group(i, wq1, 1024, N_TILE)
-            nc.scalar.copy(out=row[:, 1024:1536], in_=acc[:])
-            nc.sync.dma_start(out=out_q[0, t, :], in_=row[:])
+        def wide_out(i, first, second, out):
+            row = results.tile([P, 1024], F32, name="wide")
+            rope_out(first, row, i)
+            nc.scalar.copy(out=row[:, 512:1024], in_=second[:])
+            nc.sync.dma_start(out=out[0, P * i : P * (i + 1), 0:1024], in_=row[:])
 
-            row = new_row()
-            acc = group(i, wk, 0, N_TILE)
-            rope_out(acc, row, i)
-            acc = group(i, wk, 512, N_TILE)
-            nc.scalar.copy(out=row[:, 512:1024], in_=acc[:])
-            if i < TOKEN_TILES - 1:
-                acc = group(i, wk, 1024, N_TILE)
-                nc.scalar.copy(out=row[:, 1024:1536], in_=acc[:])
-                nc.sync.dma_start(out=out_k[0, t, :], in_=row[:])
-            else:
-                nc.sync.dma_start(out=out_k[0, t, 0:1024], in_=row[:, 0:1024])
-                acc = group(i, wk, 1024, 256)
-                nc.scalar.copy(out=row[:, 1024:1280], in_=acc[:, 0:256])
-                nc.sync.dma_start(out=out_k[0, t, 1024:1280], in_=row[:, 1024:1280])
-                acc = group(i, wk, 1280, 128)
-                nc.scalar.copy(out=row[:, 1280:1408], in_=acc[:, 0:128])
-                nc.sync.dma_start(out=out_k[0, t, 1280:1408], in_=row[:, 1280:1408])
-                acc = group(i, wk, 1408, 128)
-                nc.vector.tensor_copy(out=row[:, 1408:1536], in_=acc[:, 0:128])
-                nc.sync.dma_start(out=out_k[0, t, 1408:1536], in_=row[:, 1408:1536])
+        accs = [(new_acc(), new_acc()) for i in range(4)]
+        for g in range(PASSES):
+            for i in range(4):
+                for h in (0, 1):
+                    mx_pass(accs[i][h], i, wq0, 512 * h, N_TILE, g)
+        for i in range(4):
+            wide_out(i, accs[i][0], accs[i][1], out_q)
+
+        def wide_group(i, wblock, out):
+            first = group(i, wblock, 0, N_TILE)
+            second = group(i, wblock, 512, N_TILE)
+            wide_out(i, first, second, out)
+
+        def narrow_group(i, wblock, out):
+            pieces = ((0, 512),) if i < TOKEN_TILES - 1 or out is out_q else ((0, 256), (256, 128), (384, 128))
+            for c, n in pieces:
+                acc = group(i, wblock, c, n)
+                row = results.tile([P, n], F32, name="narrow")
+                if c == 384:
+                    nc.vector.tensor_copy(out=row[:], in_=acc[:, 0:n])
+                else:
+                    nc.scalar.copy(out=row[:], in_=acc[:, 0:n])
+                nc.sync.dma_start(out=out[0, P * i : P * (i + 1), 1024 + c : 1024 + c + n], in_=row[:])
+
+        for i in range(4, TOKEN_TILES):
+            wide_group(i, wq0, out_q)
+        for i in range(TOKEN_TILES):
+            narrow_group(i, wq1, out_q)
+        for i in range(TOKEN_TILES):
+            wide_group(i, wk0, out_k)
+        for i in range(TOKEN_TILES):
+            narrow_group(i, wk1, out_k)

import math
from contextlib import ExitStack

import concourse.mybir as mybir

F32 = mybir.dt.float32
BF16 = mybir.dt.bfloat16
I32 = mybir.dt.int32
U8 = mybir.dt.uint8
FP4X4 = mybir.dt.float4_e2m1fn_x4
ALU = mybir.AluOpType
ACT = mybir.ActivationFunctionType

P = 128
TOKENS, CHANNELS, OUT = 1536, 4096, 1536
PASSES = CHANNELS // 512
N_TILE = 512
TOKEN_TILES = TOKENS // P
ROPE = 16
PAIRS = ROPE // 2
BASE = 1e4
WARM = 10

FLOPS = 2 * TOKENS * CHANNELS * 2 * OUT


def load_codes(nc, block, words, g0, g1):
    codes, planes, c0 = block
    nbytes = codes.shape[2]
    nc.sync.dma_start(
        out=codes[:, g0:g1, :].bitcast(I32),
        in_=words[g0:g1, :, 2 * c0 : 2 * c0 + nbytes].rearrange("g p b -> p g b").bitcast(I32),
    )


def load_scales(nc, block, scales, g0, g1):
    codes, planes, c0 = block
    width = planes.shape[2]
    for q in range(4):
        nc.sync.dma_start(
            out=planes[32 * q : 32 * q + 4, g0:g1, :].bitcast(I32),
            in_=scales[g0:g1, 4 * q : 4 * q + 4, c0 : c0 + width].rearrange("g r n -> r g n").bitcast(I32),
        )


def zero_planes(engine, block, g0, g1):
    codes, planes, c0 = block
    engine.memset(planes[:, g0:g1, :].bitcast(I32), 0)


def tile_wqkv_pa_kernel(tc, q_words, q_scales, wq_words, wq_scales, wk_words, wk_scales, out_q, out_k):
    nc = tc.nc
    with ExitStack() as ctx:
        keep = ctx.enter_context(tc.tile_pool(name="keep", bufs=1))
        results = ctx.enter_context(tc.tile_pool(name="results", bufs=8))
        small = ctx.enter_context(tc.tile_pool(name="small", bufs=4))
        psum = ctx.enter_context(tc.psum_pool(name="psum", bufs=8))
        ctx.enter_context(tc.manual_schedule())

        def make_block(name, c0, width):
            codes = keep.tile([P, PASSES, 2 * width], U8, name=name + "_codes", align_bytes=256)
            planes = keep.tile([P, PASSES, width], U8, name=name + "_planes", align_bytes=256)
            return codes, planes, c0

        xs = [make_block("x" + str(n), 512 * n, 512) for n in range(3)]
        wq0 = make_block("wq0", 0, 1024)
        wq1 = make_block("wq1", 1024, 512)
        wk0 = make_block("wk0", 0, 1024)
        wk1 = make_block("wk1", 1024, 512)

        zero_planes(nc.gpsimd, xs[0], 0, 5)
        zero_planes(nc.vector, wq0, 0, 3)
        ones = keep.tile([P, N_TILE], BF16, name="ones", align_bytes=64)
        nc.vector.memset(ones[:], 1.0)
        pos = keep.tile([P, TOKEN_TILES], I32, name="pos")
        nc.gpsimd.iota(pos[:], pattern=[[P, TOKEN_TILES]], base=0, channel_multiplier=1)
        zero_planes(nc.vector, wq0, 3, 6)
        zero_planes(nc.vector, xs[0], 5, 8)
        zero_planes(nc.vector, wq0, 6, 8)
        for block in (xs[1], xs[2], wq1, wk0, wk1):
            zero_planes(nc.vector, block, 0, 8)

        def load_pair(g0, g1):
            load_codes(nc, xs[0], q_words, g0, g1)
            load_codes(nc, wq0, wq_words, g0, g1)

        load_pair(0, 1)
        load_scales(nc, xs[0], q_scales, 0, 5)
        load_scales(nc, wq0, wq_scales, 0, 3)
        load_pair(1, 2)
        load_pair(2, 4)
        load_scales(nc, wq0, wq_scales, 3, 6)
        load_pair(4, 6)
        load_scales(nc, xs[0], q_scales, 5, 8)
        load_scales(nc, wq0, wq_scales, 6, 8)
        load_pair(6, 8)
        for block, words, scales in ((xs[1], q_words, q_scales), (xs[2], q_words, q_scales), (wq1, wq_words, wq_scales), (wk0, wk_words, wk_scales), (wk1, wk_words, wk_scales)):
            load_scales(nc, block, scales, 0, 8)
            load_codes(nc, block, words, 0, 4)
            load_codes(nc, block, words, 4, 8)

        turns = keep.tile([P, 2, TOKEN_TILES, PAIRS], F32, name="turns")
        for j in range(PAIRS):
            per_pos = BASE ** (-2.0 * j / ROPE) / (2.0 * math.pi)
            nc.vector.tensor_scalar(out=turns[:, 0, :, j], in0=pos[:], scalar1=per_pos, scalar2=None, op0=ALU.mult)
        nc.vector.tensor_scalar(out=turns[:, 1, :, :], in0=turns[:, 0, :, :], scalar1=0.75, scalar2=None, op0=ALU.add)
        whole = keep.tile([P, 2, TOKEN_TILES, PAIRS], I32, name="whole")
        nc.vector.tensor_copy(out=whole[:], in_=turns[:])
        whole_f = keep.tile([P, 2, TOKEN_TILES, PAIRS], F32, name="whole_f")
        nc.vector.tensor_copy(out=whole_f[:], in_=whole[:])
        part = keep.tile([P, 2, TOKEN_TILES, PAIRS], F32, name="part")
        nc.vector.tensor_tensor(out=part[:], in0=turns[:], in1=whole_f[:], op=ALU.subtract)
        over = keep.tile([P, 2, TOKEN_TILES, PAIRS], F32, name="over")
        nc.vector.tensor_scalar(out=over[:], in0=part[:], scalar1=0.5, scalar2=None, op0=ALU.is_gt)
        near = keep.tile([P, 2, TOKEN_TILES, PAIRS], F32, name="near")
        nc.vector.tensor_tensor(out=near[:], in0=part[:], in1=over[:], op=ALU.subtract)
        dist = keep.tile([P, 2, TOKEN_TILES, PAIRS], F32, name="dist")
        nc.vector.scalar_tensor_tensor(out=dist[:], in0=near[:], scalar=-1.0, in1=near[:], op0=ALU.mult, op1=ALU.max)
        folded = keep.tile([P, 2, TOKEN_TILES, PAIRS], F32, name="folded")
        nc.vector.tensor_scalar(out=folded[:], in0=dist[:], scalar1=-1.0, scalar2=0.25, op0=ALU.mult, op1=ALU.add)
        cos = keep.tile([P, TOKEN_TILES, PAIRS, 2], F32, name="cos")
        sin = keep.tile([P, TOKEN_TILES, PAIRS, 2], F32, name="sin")
        full = 2.0 * math.pi
        nc.scalar.activation(out=cos[:, :, :, 0], in_=folded[:, 0, :, :], func=ACT.Sin, scale=full)
        nc.scalar.activation(out=cos[:, :, :, 1], in_=folded[:, 0, :, :], func=ACT.Sin, scale=full)
        nc.scalar.activation(out=sin[:, :, :, 0], in_=folded[:, 1, :, :], func=ACT.Sin, scale=-full)
        nc.scalar.activation(out=sin[:, :, :, 1], in_=folded[:, 1, :, :], func=ACT.Sin, scale=full)

        warm = psum.tile([P, N_TILE], F32, name="acc")
        for w in range(WARM):
            nc.tensor.matmul(out=warm[:], lhsT=ones[:, 0:P], rhs=ones[:], start=True, stop=True)

        def mx_pass(acc, i, wblock, c, n, g):
            xblock = xs[i // 4]
            m = P * (i % 4)
            nc.tensor.matmul_mx(
                out=acc[:, 0:n],
                lhsT=xblock[0][:, g, 2 * m : 2 * (m + P)].bitcast(FP4X4),
                lhsT_scale=xblock[1][:, g, m : m + P],
                rhs=wblock[0][:, g, 2 * c : 2 * (c + n)].bitcast(FP4X4),
                rhs_scale=wblock[1][:, g, c : c + n],
                start=(g == 0),
                stop=(g == PASSES - 1),
            )

        def rope_out(acc, row, i):
            nc.vector.tensor_copy(out=row[:, ROPE:N_TILE], in_=acc[:, ROPE:N_TILE])
            pairs = acc[:, 0:ROPE].rearrange("p (j t) -> p j t", t=2)
            straight = small.tile([P, PAIRS, 2], F32, name="straight")
            nc.vector.tensor_tensor(out=straight[:], in0=pairs, in1=cos[:, i, :, :], op=ALU.mult)
            crossed = small.tile([P, PAIRS, 2], F32, name="crossed")
            nc.vector.tensor_tensor(out=crossed[:], in0=pairs[:, :, ::-1], in1=sin[:, i, :, :], op=ALU.mult)
            nc.vector.tensor_tensor(out=row[:, 0:ROPE].rearrange("p (j t) -> p j t", t=2), in0=straight[:], in1=crossed[:], op=ALU.add)

        def new_acc():
            return psum.tile([P, N_TILE], F32, name="acc")

        def group(i, wblock, c, n):
            acc = new_acc()
            for g in range(PASSES):
                mx_pass(acc, i, wblock, c, n, g)
            return acc

        def wide_out(i, first, second, out):
            row = results.tile([P, 1024], F32, name="wide")
            rope_out(first, row, i)
            nc.scalar.copy(out=row[:, 512:1024], in_=second[:])
            nc.sync.dma_start(out=out[0, P * i : P * (i + 1), 0:1024], in_=row[:])

        accs = [(new_acc(), new_acc()) for i in range(4)]
        for g in range(PASSES):
            for i in range(4):
                for h in (0, 1):
                    mx_pass(accs[i][h], i, wq0, 512 * h, N_TILE, g)
        for i in range(4):
            wide_out(i, accs[i][0], accs[i][1], out_q)

        def wide_group(i, wblock, out):
            first = group(i, wblock, 0, N_TILE)
            second = group(i, wblock, 512, N_TILE)
            wide_out(i, first, second, out)

        def narrow_group(i, wblock, out):
            pieces = ((0, 512),) if i < TOKEN_TILES - 1 or out is out_q else ((0, 256), (256, 128), (384, 128))
            for c, n in pieces:
                acc = group(i, wblock, c, n)
                row = results.tile([P, n], F32, name="narrow")
                if c == 384:
                    nc.vector.tensor_copy(out=row[:], in_=acc[:, 0:n])
                else:
                    nc.scalar.copy(out=row[:], in_=acc[:, 0:n])
                nc.sync.dma_start(out=out[0, P * i : P * (i + 1), 1024 + c : 1024 + c + n], in_=row[:])

        for i in range(4, TOKEN_TILES):
            wide_group(i, wq0, out_q)
        for i in range(TOKEN_TILES):
            narrow_group(i, wq1, out_q)
        for i in range(TOKEN_TILES):
            wide_group(i, wk0, out_k)
        for i in range(TOKEN_TILES):
            narrow_group(i, wk1, out_k)
